import numpy as np
import ml_dtypes


def mxq(x, axis, fmt="e4m3"):
    dtype, down = {"e4m3": (ml_dtypes.float8_e4m3fn, 7), "e5m2": (ml_dtypes.float8_e5m2, 14)}[fmt]
    v = np.moveaxis(np.asarray(x, np.float32).astype(ml_dtypes.bfloat16).astype(np.float64), axis, -1)
    blocks = v.reshape(v.shape[:-1] + (-1, 32))
    amax = np.abs(blocks).max(-1, keepdims=True)
    byte = np.maximum(np.where(amax > 0, np.frexp(amax)[1] - 1 + 127, 0) - down, 1)
    scale = np.exp2(byte - 127.0)
    codes = (blocks / scale).astype(np.float32).astype(dtype).astype(np.float64)
    return np.moveaxis((codes * scale).reshape(v.shape), -1, axis)


WIDE = False


def mx_kscale(k):
    if not WIDE:
        return np.ones(k)
    levels = np.array([10, -10, 5, -5, 0])
    a = np.random.permutation(np.resize(levels, k // 512 * 4)).reshape(k // 512, 4)
    idx = np.arange(k)
    return np.exp2(a[idx // 512, idx % 128 // 32])


BF16 = ml_dtypes.bfloat16


def bf(x):
    return np.asarray(x, np.float32).astype(BF16)


def f64(x):
    return np.asarray(x).astype(np.float64)


B, S, D, H, DK = 4, 128, 8192, 16, 32
E = H * DK
HALF = DK // 2


def rope(t, cos2, sin2):
    t_even = t[..., 0::2]
    t_odd = t[..., 1::2]
    rot = np.stack([-t_odd, t_even], axis=-1).reshape(t.shape)
    return t * cos2 + rot * sin2


def setup_inputs():
    s = mx_kscale(D)
    ang = np.random.uniform(-np.pi, np.pi, (S, HALF))
    return {"x": bf(np.random.standard_normal((B, S, D)) * s),
            "Wq": bf(np.random.standard_normal((D, E)) / np.sqrt(D) / s[:, None]),
            "Wk": bf(np.random.standard_normal((D, E)) / np.sqrt(D) / s[:, None]),
            "cos2": bf(np.repeat(np.cos(ang), 2, axis=-1)),
            "sin2": bf(np.repeat(np.sin(ang), 2, axis=-1))}


def reference(x, Wq, Wk, cos2, sin2):
    xq = mxq(f64(x), 2, "e4m3")
    q = (xq @ mxq(f64(Wq), 0, "e4m3")).reshape(B, S, H, DK).swapaxes(1, 2)
    k = (xq @ mxq(f64(Wk), 0, "e4m3")).reshape(B, S, H, DK).swapaxes(1, 2)
    c, sn = f64(cos2), f64(sin2)
    return rope(q, c, sn), rope(k, c, sn)

@@ -1,0 +1,201 @@
+from contextlib import ExitStack
+
+import concourse.mybir as mybir
+from concourse.masks import make_identity
+
+F32 = mybir.dt.float32
+BF16 = mybir.dt.bfloat16
+U32 = mybir.dt.uint32
+U8 = mybir.dt.uint8
+FP8X4 = mybir.dt.float8_e4m3fn_x4
+MULT = mybir.AluOpType.mult
+ADD = mybir.AluOpType.add
+
+B, S, D, H, DK = 4, 128, 8192, 16, 32
+E = H * DK
+HALF = DK // 2
+
+P = 128
+PACK = 4
+K_PASS = P * PACK
+PASSES = D // K_PASS
+PSUM_BANKS = 8
+
+X_LOAD_PASSES = 8
+BANK_PASSES = 2
+QUANT_PASSES = 4
+BUNCH = 2
+BUNCHES = PASSES // BUNCH
+
+VECTOR_COLS_Q = 240
+VECTOR_COLS_K = 176
+
+FLOPS = 2 * B * S * D * 2 * E
+
+
+def tile_multiheadselfattention_pa_k_kernel(tc, x, Wq, Wk, cos2, sin2, out_0, out_1):
+    nc = tc.nc
+    with ExitStack() as ctx:
+        const = ctx.enter_context(tc.tile_pool(name="const", bufs=1))
+        keep = ctx.enter_context(tc.tile_pool(name="keep", bufs=1))
+        x_pool = ctx.enter_context(tc.tile_pool(name="x_raw", bufs=4))
+        w_pool = ctx.enter_context(tc.tile_pool(name="w_raw", bufs=6))
+        grouped_pool = ctx.enter_context(tc.tile_pool(name="grouped", bufs=4))
+        w_mx_pool = ctx.enter_context(tc.tile_pool(name="w_mx", bufs=6))
+        rope_pool = ctx.enter_context(tc.tile_pool(name="rope", bufs=2))
+        out_pool = ctx.enter_context(tc.tile_pool(name="rotated", bufs=2 * B))
+        banks = ctx.enter_context(tc.psum_pool(name="banks", bufs=PSUM_BANKS))
+        ctx.enter_context(tc.manual_schedule())
+
+        identity = const.tile([P, P], F32)
+        make_identity(nc, identity[:])
+        cos_bf = const.tile([P, DK], BF16)
+        sin_bf = const.tile([P, DK], BF16)
+        nc.scalar.dma_start(out=cos_bf[:], in_=cos2)
+        nc.scalar.dma_start(out=sin_bf[:], in_=sin2)
+        cos_pairs = cos_bf[:].rearrange("p (j r) -> p r j", r=2)
+        sin_pairs = sin_bf[:].rearrange("p (j r) -> p r j", r=2)
+        factor = const.tile([P, 2, 2, HALF], F32)
+        nc.vector.tensor_copy(out=factor[:, 0, 0, :], in_=cos_pairs[:, 0, :])
+        nc.vector.tensor_copy(out=factor[:, 0, 1, :], in_=sin_pairs[:, 1, :])
+        nc.vector.tensor_scalar_mul(out=factor[:, 1, 0, :], in0=sin_pairs[:, 0, :], scalar1=-1.0)
+        nc.vector.tensor_copy(out=factor[:, 1, 1, :], in_=cos_pairs[:, 1, :])
+
+        x_codes = keep.tile([P, B, PASSES, S], U32, align_bytes=64)
+        x_scales = keep.tile([P, B, PASSES, S], U8, align_bytes=64)
+
+        def transpose_bank(x_words, first_pass):
+            xt = banks.tile([P, BANK_PASSES, 2, S], F32, name="xt", tag="bank")
+            for i in range(BANK_PASSES):
+                for u in range(2):
+                    nc.tensor.transpose(xt[:, i, u, :], x_words[:, first_pass + i, u, :], identity[:])
+            return xt
+
+        def quantise_x(x_grouped, b, first_pass):
+            nc.vector.quantize_mx(
+                out=x_codes[:, b, first_pass : first_pass + QUANT_PASSES, :]
+                .rearrange("p g s -> p (g s)")
+                .bitcast(FP8X4),
+                scales=x_scales[:, b, first_pass : first_pass + QUANT_PASSES, :].rearrange(
+                    "p g s -> p (g s)"
+                ),
+                in_=x_grouped[:].rearrange("p g s t -> p (g s t)"),
+            )
+
+        previous = None
+        for b in range(B):
+            for load in range(PASSES // X_LOAD_PASSES):
+                x_raw = x_pool.tile([P, X_LOAD_PASSES * K_PASS], BF16)
+                first_k = load * X_LOAD_PASSES * K_PASS
+                nc.sync.dma_start(
+                    out=x_raw[:], in_=x[b][:, first_k : first_k + X_LOAD_PASSES * K_PASS]
+                )
+                x_words = x_raw[:].bitcast(F32).rearrange("s (g p u) -> s g u p", p=P, u=2)
+                for group in range(X_LOAD_PASSES // QUANT_PASSES):
+                    x_grouped = grouped_pool.tile([P, QUANT_PASSES, S, PACK], BF16, align_bytes=64)
+                    grouped_words = x_grouped[:].bitcast(F32)
+                    for i in range(0, QUANT_PASSES, BANK_PASSES):
+                        xt = transpose_bank(x_words, group * QUANT_PASSES + i)
+                        nc.scalar.copy(
+                            out=grouped_words[:, i : i + BANK_PASSES, :, :],
+                            in_=xt[:].rearrange("p g u s -> p g s u"),
+                        )
+                    if previous is not None:
+                        quantise_x(*previous)
+                    previous = (x_grouped, b, load * X_LOAD_PASSES + group * QUANT_PASSES)
+        quantise_x(*previous)
+
+        def prepare_w(w, bunch, vector_cols):
+            w_raw = w_pool.tile([P, BUNCH, PACK, E], BF16)
+            nc.sync.dma_start(
+                out=w_raw[:].rearrange("p g t n -> p g (t n)"),
+                in_=w.rearrange("(g p t) n -> p g (t n)", p=P, t=PACK)[
+                    :, bunch * BUNCH : (bunch + 1) * BUNCH, :
+                ],
+            )
+            grouped = []
+            for i in range(BUNCH):
+                w_grouped = grouped_pool.tile([P, E, PACK], BF16, align_bytes=64)
+                nc.vector.tensor_copy(
+                    out=w_grouped[:, :vector_cols, :].rearrange("p (c i) t -> p c t i", i=4),
+                    in_=w_raw[:, i, :, :vector_cols].rearrange("p t (c i) -> p c t i", i=4),
+                )
+                nc.scalar.copy(
+                    out=w_grouped[:, vector_cols:, :].rearrange("p (c i) t -> p c t i", i=4),
+                    in_=w_raw[:, i, :, vector_cols:].rearrange("p t (c i) -> p c t i", i=4),
+                )
+                grouped.append(w_grouped)
+            w_mx = []
+            for i in range(BUNCH):
+                w_codes = w_mx_pool.tile([P, E], U32, align_bytes=64)
+                w_scales = w_mx_pool.tile([P, E], U8, align_bytes=64)
+                nc.vector.quantize_mx(
+                    out=w_codes[:].bitcast(FP8X4),
+                    scales=w_scales[:],
+                    in_=grouped[i][:].rearrange("p n t -> p (n t)"),
+                )
+                w_mx.append((w_codes, w_scales))
+            return w_mx
+
+        def multiply(acc, bunch, w_mx):
+            for b in range(B):
+                for i in range(BUNCH):
+                    g = bunch * BUNCH + i
+                    nc.tensor.matmul_mx(
+                        out=acc[b][:],
+                        lhsT=x_codes[:, b, g, :].bitcast(FP8X4),
+                        lhsT_scale=x_scales[:, b, g, :],
+                        rhs=w_mx[i][0][:].bitcast(FP8X4),
+                        rhs_scale=w_mx[i][1][:],
+                        start=(g == 0),
+                        stop=(g == PASSES - 1),
+                    )
+
+        def rotation_products(acc_b):
+            products = rope_pool.tile([P, 2, 2, H, HALF], F32)
+            nc.vector.tensor_tensor(
+                out=products[:],
+                in0=acc_b[:]
+                .rearrange("p (h j w) -> p w h j", h=H, w=2)
+                .unsqueeze(2)
+                .to_broadcast([P, 2, 2, H, HALF]),
+                in1=factor[:].unsqueeze(3).to_broadcast([P, 2, 2, H, HALF]),
+                op=MULT,
+            )
+            return products
+
+        def rotation_sum(products):
+            rotated = out_pool.tile([P, H, DK], F32)
+            nc.vector.tensor_tensor(
+                out=rotated[:].rearrange("p h (j r) -> p h j r", r=2),
+                in0=products[:, 0].rearrange("p r h j -> p h j r"),
+                in1=products[:, 1].rearrange("p r h j -> p h j r"),
+                op=ADD,
+            )
+            return rotated
+
+        def store(out, b, rotated):
+            nc.sync.dma_start(out=out[b].rearrange("h s d -> s h d"), in_=rotated[:])
+
+        q_acc = [banks.tile([P, E], F32, name="q_acc%d" % b, tag="bank") for b in range(B)]
+        for bunch in range(BUNCHES):
+            multiply(q_acc, bunch, prepare_w(Wq, bunch, VECTOR_COLS_Q))
+
+        k_acc = [banks.tile([P, E], F32, name="k_acc%d" % b, tag="bank") for b in range(B)]
+        q_rotated = []
+        products = None
+        for bunch in range(BUNCHES):
+            multiply(k_acc, bunch, prepare_w(Wk, bunch, VECTOR_COLS_K))
+            if bunch % 2 == 0:
+                products = rotation_products(q_acc[bunch // 2])
+            else:
+                q_rotated.append(rotation_sum(products))
+
+        for b in range(B):
+            store(out_0, b, q_rotated[b])
+        k_products = []
+        for b in range(B):
+            k_products.append(rotation_products(k_acc[b]))
+            if b > 0:
+                store(out_1, b - 1, rotation_sum(k_products[b - 1]))
+        store(out_1, B - 1, rotation_sum(k_products[B - 1]))

@@ -90,7 +90,7 @@ def tile_multiheadselfattention_pa_k_kernel(tc, x, Wq, Wk, cos2, sin2, out_0, ou
                 nc.sync.dma_start(
                     out=x_raw[:], in_=x[b][:, first_k : first_k + X_LOAD_PASSES * K_PASS]
                 )
-                x_words = x_raw[:].bitcast(F32).rearrange("s (g p u) -> s g u p", p=P, u=2)
+                x_words = x_raw[:].bitcast(F32).rearrange("s (g u p) -> s g u p", p=P, u=2)
                 for group in range(X_LOAD_PASSES // QUANT_PASSES):
                     x_grouped = grouped_pool.tile([P, QUANT_PASSES, S, PACK], BF16, align_bytes=64)
                     grouped_words = x_grouped[:].bitcast(F32)
@@ -108,9 +108,9 @@ def tile_multiheadselfattention_pa_k_kernel(tc, x, Wq, Wk, cos2, sin2, out_0, ou
         def prepare_w(w, bunch, vector_cols):
             w_raw = w_pool.tile([P, BUNCH, PACK, E], BF16)
             nc.sync.dma_start(
-                out=w_raw[:].rearrange("p g t n -> p g (t n)"),
-                in_=w.rearrange("(g p t) n -> p g (t n)", p=P, t=PACK)[
-                    :, bunch * BUNCH : (bunch + 1) * BUNCH, :
+                out=w_raw[:].rearrange("p g (u e) n -> p (g u) (e n)", e=2),
+                in_=w.rearrange("(m p e) n -> p m (e n)", p=P, e=2)[
+                    :, 2 * bunch * BUNCH : 2 * (bunch + 1) * BUNCH, :
                 ],
             )
             grouped = []

@@ -21,14 +21,18 @@ K_PASS = P * PACK
 PASSES = D // K_PASS
 PSUM_BANKS = 8
 
-X_LOAD_PASSES = 8
+J = B * S // P
+X_PASSES = 8
+X_LOADS = PASSES // X_PASSES
 BANK_PASSES = 2
 QUANT_PASSES = 4
-BUNCH = 2
-BUNCHES = PASSES // BUNCH
+W_PASSES = 2
+EARLY_AFTER = (2, 4, 6)
 
-VECTOR_COLS_Q = 240
-VECTOR_COLS_K = 176
+VECTOR_COLS_Q = 272
+VECTOR_COLS_EARLY_Q = 352
+VECTOR_COLS_K = 168
+ROTATE_PASSES = [3 + 3 * step // 2 for step in range(8)]
 
 FLOPS = 2 * B * S * D * 2 * E
 
@@ -40,162 +44,221 @@ def tile_multiheadselfattention_pa_k_kernel(tc, x, Wq, Wk, cos2, sin2, out_0, ou
         keep = ctx.enter_context(tc.tile_pool(name="keep", bufs=1))
         x_pool = ctx.enter_context(tc.tile_pool(name="x_raw", bufs=4))
         w_pool = ctx.enter_context(tc.tile_pool(name="w_raw", bufs=6))
-        grouped_pool = ctx.enter_context(tc.tile_pool(name="grouped", bufs=4))
-        w_mx_pool = ctx.enter_context(tc.tile_pool(name="w_mx", bufs=6))
-        rope_pool = ctx.enter_context(tc.tile_pool(name="rope", bufs=2))
-        out_pool = ctx.enter_context(tc.tile_pool(name="rotated", bufs=2 * B))
+        x_grouped_pool = ctx.enter_context(tc.tile_pool(name="x_grouped", bufs=4))
+        w_grouped_pool = ctx.enter_context(tc.tile_pool(name="w_grouped", bufs=6))
+        w_mx_pool = ctx.enter_context(tc.tile_pool(name="w_mx", bufs=8))
+        rope_pool = ctx.enter_context(tc.tile_pool(name="rope", bufs=4))
+        out_pool = ctx.enter_context(tc.tile_pool(name="rotated", bufs=2))
         banks = ctx.enter_context(tc.psum_pool(name="banks", bufs=PSUM_BANKS))
         ctx.enter_context(tc.manual_schedule())
 
         identity = const.tile([P, P], F32)
         make_identity(nc, identity[:])
-        cos_bf = const.tile([P, DK], BF16)
-        sin_bf = const.tile([P, DK], BF16)
-        nc.scalar.dma_start(out=cos_bf[:], in_=cos2)
-        nc.scalar.dma_start(out=sin_bf[:], in_=sin2)
-        cos_pairs = cos_bf[:].rearrange("p (j r) -> p r j", r=2)
-        sin_pairs = sin_bf[:].rearrange("p (j r) -> p r j", r=2)
-        factor = const.tile([P, 2, 2, HALF], F32)
-        nc.vector.tensor_copy(out=factor[:, 0, 0, :], in_=cos_pairs[:, 0, :])
-        nc.vector.tensor_copy(out=factor[:, 0, 1, :], in_=sin_pairs[:, 1, :])
-        nc.vector.tensor_scalar_mul(out=factor[:, 1, 0, :], in0=sin_pairs[:, 0, :], scalar1=-1.0)
-        nc.vector.tensor_copy(out=factor[:, 1, 1, :], in_=cos_pairs[:, 1, :])
+        permutation = const.tile([P, P], F32)
+        nc.gpsimd.tensor_copy(
+            out=permutation[:].rearrange("p (i b) -> p b i", b=B),
+            in_=identity[:].rearrange("p (b i) -> p b i", b=B),
+        )
+        cos_bf = const.tile([P, J, DK], BF16)
+        sin_bf = const.tile([P, J, DK], BF16)
+        for b in range(B):
+            for table, source in ((cos_bf, cos2), (sin_bf, sin2)):
+                nc.gpsimd.dma_start(
+                    out=table[b::B].rearrange("p j d -> p (j d)"),
+                    in_=source.rearrange("(i j) d -> i (j d)", j=J),
+                )
+        factor = const.tile([P, J, 2, DK], F32)
 
-        x_codes = keep.tile([P, B, PASSES, S], U32, align_bytes=64)
-        x_scales = keep.tile([P, B, PASSES, S], U8, align_bytes=64)
+        def make_factor():
+            parts = factor[:].rearrange("p j w (i r) -> p j w r i", r=2)
+            cos_pairs = cos_bf[:].rearrange("p j (i r) -> p j r i", r=2)
+            sin_pairs = sin_bf[:].rearrange("p j (i r) -> p j r i", r=2)
+            nc.vector.tensor_copy(out=parts[:, :, 0, 0, :], in_=cos_pairs[:, :, 0, :])
+            nc.vector.tensor_copy(out=parts[:, :, 0, 1, :], in_=sin_pairs[:, :, 1, :])
+            nc.vector.tensor_scalar_mul(
+                out=parts[:, :, 1, 0, :], in0=sin_pairs[:, :, 0, :], scalar1=-1.0
+            )
+            nc.vector.tensor_copy(out=parts[:, :, 1, 1, :], in_=cos_pairs[:, :, 1, :])
+
+        x_codes = keep.tile([P, J, PASSES, P], U32, align_bytes=64)
+        x_scales = keep.tile([P, J, PASSES, P], U8, align_bytes=64)
+
+        x_rows = x.rearrange("b s k -> (b s) k").rearrange("(p j) k -> p j k", j=J)
 
         def transpose_bank(x_words, first_pass):
-            xt = banks.tile([P, BANK_PASSES, 2, S], F32, name="xt", tag="bank")
+            xt = banks.tile([P, BANK_PASSES, 2, P], F32, name="xt", tag="bank")
             for i in range(BANK_PASSES):
                 for u in range(2):
-                    nc.tensor.transpose(xt[:, i, u, :], x_words[:, first_pass + i, u, :], identity[:])
+                    nc.tensor.transpose(
+                        xt[:, i, u, :], x_words[:, first_pass + i, u, :], permutation[:]
+                    )
             return xt
 
-        def quantise_x(x_grouped, b, first_pass):
+        def quantise_x(x_grouped, j, first_pass):
+            passes = slice(first_pass, first_pass + QUANT_PASSES)
             nc.vector.quantize_mx(
-                out=x_codes[:, b, first_pass : first_pass + QUANT_PASSES, :]
-                .rearrange("p g s -> p (g s)")
-                .bitcast(FP8X4),
-                scales=x_scales[:, b, first_pass : first_pass + QUANT_PASSES, :].rearrange(
-                    "p g s -> p (g s)"
-                ),
+                out=x_codes[:, j, passes].rearrange("p g s -> p (g s)").bitcast(FP8X4),
+                scales=x_scales[:, j, passes].rearrange("p g s -> p (g s)"),
                 in_=x_grouped[:].rearrange("p g s t -> p (g s t)"),
             )
 
-        previous = None
-        for b in range(B):
-            for load in range(PASSES // X_LOAD_PASSES):
-                x_raw = x_pool.tile([P, X_LOAD_PASSES * K_PASS], BF16)
-                first_k = load * X_LOAD_PASSES * K_PASS
-                nc.sync.dma_start(
-                    out=x_raw[:], in_=x[b][:, first_k : first_k + X_LOAD_PASSES * K_PASS]
+        def group_w(w_raw, i, vector_cols):
+            w_grouped = w_grouped_pool.tile([P, E, PACK], BF16, align_bytes=64)
+            for copy, cols in (
+                (nc.scalar.copy, slice(vector_cols, E)),
+                (nc.vector.tensor_copy, slice(0, vector_cols)),
+            ):
+                copy(
+                    out=w_grouped[:, cols, :].rearrange("p (c i) t -> p c t i", i=4),
+                    in_=w_raw[:, i, :, cols].rearrange("p t (c i) -> p c t i", i=4),
                 )
-                x_words = x_raw[:].bitcast(F32).rearrange("s (g u p) -> s g u p", p=P, u=2)
-                for group in range(X_LOAD_PASSES // QUANT_PASSES):
-                    x_grouped = grouped_pool.tile([P, QUANT_PASSES, S, PACK], BF16, align_bytes=64)
-                    grouped_words = x_grouped[:].bitcast(F32)
-                    for i in range(0, QUANT_PASSES, BANK_PASSES):
-                        xt = transpose_bank(x_words, group * QUANT_PASSES + i)
-                        nc.scalar.copy(
-                            out=grouped_words[:, i : i + BANK_PASSES, :, :],
-                            in_=xt[:].rearrange("p g u s -> p g s u"),
-                        )
-                    if previous is not None:
-                        quantise_x(*previous)
-                    previous = (x_grouped, b, load * X_LOAD_PASSES + group * QUANT_PASSES)
-        quantise_x(*previous)
+            return w_grouped
 
-        def prepare_w(w, bunch, vector_cols):
-            w_raw = w_pool.tile([P, BUNCH, PACK, E], BF16)
-            nc.sync.dma_start(
-                out=w_raw[:].rearrange("p g (u e) n -> p (g u) (e n)", e=2),
-                in_=w.rearrange("(m p e) n -> p m (e n)", p=P, e=2)[
-                    :, 2 * bunch * BUNCH : 2 * (bunch + 1) * BUNCH, :
-                ],
+        def quantise_w(w_grouped):
+            w_codes = w_mx_pool.tile([P, E], U32, align_bytes=64)
+            w_scales = w_mx_pool.tile([P, E], U8, align_bytes=64)
+            nc.vector.quantize_mx(
+                out=w_codes[:].bitcast(FP8X4),
+                scales=w_scales[:],
+                in_=w_grouped[:].rearrange("p n t -> p (n t)"),
             )
-            grouped = []
-            for i in range(BUNCH):
-                w_grouped = grouped_pool.tile([P, E, PACK], BF16, align_bytes=64)
-                nc.vector.tensor_copy(
-                    out=w_grouped[:, :vector_cols, :].rearrange("p (c i) t -> p c t i", i=4),
-                    in_=w_raw[:, i, :, :vector_cols].rearrange("p t (c i) -> p c t i", i=4),
-                )
-                nc.scalar.copy(
-                    out=w_grouped[:, vector_cols:, :].rearrange("p (c i) t -> p c t i", i=4),
-                    in_=w_raw[:, i, :, vector_cols:].rearrange("p t (c i) -> p c t i", i=4),
-                )
-                grouped.append(w_grouped)
-            w_mx = []
-            for i in range(BUNCH):
-                w_codes = w_mx_pool.tile([P, E], U32, align_bytes=64)
-                w_scales = w_mx_pool.tile([P, E], U8, align_bytes=64)
-                nc.vector.quantize_mx(
-                    out=w_codes[:].bitcast(FP8X4),
-                    scales=w_scales[:],
-                    in_=grouped[i][:].rearrange("p n t -> p (n t)"),
-                )
-                w_mx.append((w_codes, w_scales))
-            return w_mx
+            return w_codes, w_scales
 
-        def multiply(acc, bunch, w_mx):
-            for b in range(B):
-                for i in range(BUNCH):
-                    g = bunch * BUNCH + i
-                    nc.tensor.matmul_mx(
-                        out=acc[b][:],
-                        lhsT=x_codes[:, b, g, :].bitcast(FP8X4),
-                        lhsT_scale=x_scales[:, b, g, :],
-                        rhs=w_mx[i][0][:].bitcast(FP8X4),
-                        rhs_scale=w_mx[i][1][:],
-                        start=(g == 0),
-                        stop=(g == PASSES - 1),
-                    )
+        def multiply(acc, g, w_codes, w_scales):
+            for j in range(J):
+                nc.tensor.matmul_mx(
+                    out=acc[j][:],
+                    lhsT=x_codes[:, j, g, :].bitcast(FP8X4),
+                    lhsT_scale=x_scales[:, j, g, :],
+                    rhs=w_codes[:].bitcast(FP8X4),
+                    rhs_scale=w_scales[:],
+                    start=(g == 0),
+                    stop=(g == PASSES - 1),
+                )
 
-        def rotation_products(acc_b):
-            products = rope_pool.tile([P, 2, 2, H, HALF], F32)
+        def rotation_products(acc, j, heads):
+            n = heads.stop - heads.start
+            products = rope_pool.tile([P, 2, n, DK], F32, name="products")
             nc.vector.tensor_tensor(
-                out=products[:],
-                in0=acc_b[:]
-                .rearrange("p (h j w) -> p w h j", h=H, w=2)
+                out=products[:].rearrange("p w h (i r) -> p w h i r", r=2),
+                in0=acc[j][:, heads.start * DK : heads.stop * DK]
+                .rearrange("p (h i w) -> p w h i", h=n, w=2)
+                .unsqueeze(4)
+                .to_broadcast([P, 2, n, HALF, 2]),
+                in1=factor[:, j]
                 .unsqueeze(2)
-                .to_broadcast([P, 2, 2, H, HALF]),
-                in1=factor[:].unsqueeze(3).to_broadcast([P, 2, 2, H, HALF]),
+                .to_broadcast([P, 2, n, DK])
+                .rearrange("p w h (i r) -> p w h i r", r=2),
                 op=MULT,
             )
             return products
 
-        def rotation_sum(products):
-            rotated = out_pool.tile([P, H, DK], F32)
-            nc.vector.tensor_tensor(
-                out=rotated[:].rearrange("p h (j r) -> p h j r", r=2),
-                in0=products[:, 0].rearrange("p r h j -> p h j r"),
-                in1=products[:, 1].rearrange("p r h j -> p h j r"),
-                op=ADD,
+        def rotation_sum(engine, rotated, j, heads, products):
+            engine.tensor_tensor(
+                out=rotated[:, heads, j, :], in0=products[:, 0], in1=products[:, 1], op=ADD
             )
-            return rotated
 
-        def store(out, b, rotated):
-            nc.sync.dma_start(out=out[b].rearrange("h s d -> s h d"), in_=rotated[:])
+        def store(out, heads, rotated):
+            for b in range(B):
+                nc.sync.dma_start(
+                    out=out[b, heads].rearrange("h (i j) d -> i h (j d)", j=J),
+                    in_=rotated[b::B, heads].rearrange("p h j d -> p h (j d)"),
+                )
 
-        q_acc = [banks.tile([P, E], F32, name="q_acc%d" % b, tag="bank") for b in range(B)]
-        for bunch in range(BUNCHES):
-            multiply(q_acc, bunch, prepare_w(Wq, bunch, VECTOR_COLS_Q))
+        all_heads = slice(0, H)
+        q_rotated = out_pool.tile([P, H, J, DK], F32, name="q_rotated", tag="rotated")
+        q_products = []
 
-        k_acc = [banks.tile([P, E], F32, name="k_acc%d" % b, tag="bank") for b in range(B)]
-        q_rotated = []
-        products = None
-        for bunch in range(BUNCHES):
-            multiply(k_acc, bunch, prepare_w(Wk, bunch, VECTOR_COLS_K))
-            if bunch % 2 == 0:
-                products = rotation_products(q_acc[bunch // 2])
+        def rotate_q(step):
+            j = step // 2
+            if step % 2 == 0:
+                q_products.append(rotation_products(q_acc, j, all_heads))
             else:
-                q_rotated.append(rotation_sum(products))
+                rotation_sum(nc.vector, q_rotated, j, all_heads, q_products[j])
 
-        for b in range(B):
-            store(out_0, b, q_rotated[b])
-        k_products = []
-        for b in range(B):
-            k_products.append(rotation_products(k_acc[b]))
-            if b > 0:
-                store(out_1, b - 1, rotation_sum(k_products[b - 1]))
-        store(out_1, B - 1, rotation_sum(k_products[B - 1]))
+        quantise_before = []
+        ready = []
+
+        def quantise_next():
+            while quantise_before:
+                quantise_before.pop(0)()
+
+        def x_unit(j, load):
+            x_raw = x_pool.tile([P, X_PASSES * K_PASS], BF16)
+            pieces = X_PASSES // BANK_PASSES if j == 0 and load == 0 else 1
+            width = X_PASSES * K_PASS // pieces
+            for piece in range(pieces):
+                first_k = load * X_PASSES * K_PASS + piece * width
+                nc.sync.dma_start(
+                    out=x_raw[:, piece * width : (piece + 1) * width],
+                    in_=x_rows[:, j, first_k : first_k + width],
+                )
+            x_words = x_raw[:].bitcast(F32).rearrange("s (g p u) -> s g u p", p=P, u=2)
+            for first in range(0, X_PASSES, QUANT_PASSES):
+                x_grouped = x_grouped_pool.tile([P, QUANT_PASSES, P, PACK], BF16, align_bytes=64)
+                for i in range(0, QUANT_PASSES, BANK_PASSES):
+                    xt = transpose_bank(x_words, first + i)
+                    nc.scalar.copy(
+                        out=x_grouped[:].bitcast(F32)[:, i : i + BANK_PASSES],
+                        in_=xt[:].rearrange("p g u s -> p g s u"),
+                    )
+                quantise_next()
+                quantise_before.append(lambda a=x_grouped, b=load * X_PASSES + first: quantise_x(a, j, b))
+
+        def w_unit(w, acc, first, vector_cols, rotate):
+            w_raw = w_pool.tile([P, W_PASSES, PACK, E], BF16)
+            nc.sync.dma_start(
+                out=w_raw[:].rearrange("p g t n -> p g (t n)"),
+                in_=w.rearrange("(g p t) n -> p g (t n)", p=P, t=PACK)[:, first : first + W_PASSES, :],
+            )
+            for i in range(W_PASSES):
+                g = first + i
+                w_grouped = group_w(w_raw, i, vector_cols)
+                quantise_next()
+                quantise_before.append(lambda a=w_grouped, b=g: ready.append((b, *quantise_w(a))))
+                if acc is not None:
+                    while ready:
+                        multiply(acc, *ready.pop(0))
+                rotate(g)
+
+        early = 0
+        for n in range(J * X_LOADS):
+            x_unit(n // X_LOADS, n % X_LOADS)
+            if n in EARLY_AFTER:
+                w_unit(Wq, None, early, VECTOR_COLS_EARLY_Q, lambda g: None)
+                early += W_PASSES
+        q_acc = [banks.tile([P, E], F32, name="q_acc%d" % j, tag="bank") for j in range(J)]
+        k_acc = [banks.tile([P, E], F32, name="k_acc%d" % j, tag="bank") for j in range(J)]
+        for first in range(early, PASSES, W_PASSES):
+            w_unit(Wq, q_acc, first, VECTOR_COLS_Q, lambda g: None)
+        quantise_next()
+        multiply(q_acc, *ready.pop(0))
+
+        def rotate_k_pass(g):
+            if g == 0:
+                make_factor()
+            if g in ROTATE_PASSES:
+                rotate_q(ROTATE_PASSES.index(g))
+
+        for first in range(0, PASSES, W_PASSES):
+            w_unit(Wk, k_acc, first, VECTOR_COLS_K, rotate_k_pass)
+        quantise_next()
+        multiply(k_acc, *ready.pop(0))
+
+        store(out_0, all_heads, q_rotated)
+        k_rotated = out_pool.tile([P, H, J, DK], F32, name="k_rotated", tag="rotated")
+        halves = (slice(0, H // 2), slice(H // 2, H))
+        vector_sums = []
+        for half, heads in enumerate(halves):
+            for j in range(J):
+                products = rotation_products(k_acc, j, heads)
+                if vector_sums:
+                    rotation_sum(nc.vector, k_rotated, *vector_sums.pop(0))
+                if half == 1 and j == 0:
+                    store(out_1, halves[0], k_rotated)
+                if j < J - 2 * half:
+                    rotation_sum(nc.gpsimd, k_rotated, j, heads, products)
+                else:
+                    vector_sums.append((j, heads, products))
+        rotation_sum(nc.vector, k_rotated, *vector_sums.pop(0))
+        store(out_1, halves[1], k_rotated)

@@ -27,12 +27,12 @@ X_LOADS = PASSES // X_PASSES
 BANK_PASSES = 2
 QUANT_PASSES = 4
 W_PASSES = 2
-EARLY_AFTER = (2, 4, 6)
+EARLY_AFTER = (3, 6)
 
-VECTOR_COLS_Q = 272
-VECTOR_COLS_EARLY_Q = 352
-VECTOR_COLS_K = 168
-ROTATE_PASSES = [3 + 3 * step // 2 for step in range(8)]
+VECTOR_COLS_Q = 256
+VECTOR_COLS_EARLY_Q = 320
+VECTOR_COLS_K = 176
+ROTATE_PASS = 3
 
 FLOPS = 2 * B * S * D * 2 * E
 
@@ -67,18 +67,15 @@ def tile_multiheadselfattention_pa_k_kernel(tc, x, Wq, Wk, cos2, sin2, out_0, ou
                     out=table[b::B].rearrange("p j d -> p (j d)"),
                     in_=source.rearrange("(i j) d -> i (j d)", j=J),
                 )
-        factor = const.tile([P, J, 2, DK], F32)
+        cos = const.tile([P, J, DK], F32)
+        sin = const.tile([P, J, DK], F32)
 
-        def make_factor():
-            parts = factor[:].rearrange("p j w (i r) -> p j w r i", r=2)
-            cos_pairs = cos_bf[:].rearrange("p j (i r) -> p j r i", r=2)
-            sin_pairs = sin_bf[:].rearrange("p j (i r) -> p j r i", r=2)
-            nc.vector.tensor_copy(out=parts[:, :, 0, 0, :], in_=cos_pairs[:, :, 0, :])
-            nc.vector.tensor_copy(out=parts[:, :, 0, 1, :], in_=sin_pairs[:, :, 1, :])
-            nc.vector.tensor_scalar_mul(
-                out=parts[:, :, 1, 0, :], in0=sin_pairs[:, :, 0, :], scalar1=-1.0
-            )
-            nc.vector.tensor_copy(out=parts[:, :, 1, 1, :], in_=cos_pairs[:, :, 1, :])
+        def make_tables():
+            nc.vector.tensor_copy(out=cos[:], in_=cos_bf[:])
+            pairs = sin[:].rearrange("p j (i r) -> p j r i", r=2)
+            pairs_bf = sin_bf[:].rearrange("p j (i r) -> p j r i", r=2)
+            nc.vector.tensor_scalar_mul(out=pairs[:, :, 0, :], in0=pairs_bf[:, :, 0, :], scalar1=-1.0)
+            nc.vector.tensor_copy(out=pairs[:, :, 1, :], in_=pairs_bf[:, :, 1, :])
 
         x_codes = keep.tile([P, J, PASSES, P], U32, align_bytes=64)
         x_scales = keep.tile([P, J, PASSES, P], U8, align_bytes=64)
@@ -139,16 +136,17 @@ def tile_multiheadselfattention_pa_k_kernel(tc, x, Wq, Wk, cos2, sin2, out_0, ou
         def rotation_products(acc, j, heads):
             n = heads.stop - heads.start
             products = rope_pool.tile([P, 2, n, DK], F32, name="products")
+            sums = acc[j][:, heads.start * DK : heads.stop * DK]
             nc.vector.tensor_tensor(
-                out=products[:].rearrange("p w h (i r) -> p w h i r", r=2),
-                in0=acc[j][:, heads.start * DK : heads.stop * DK]
-                .rearrange("p (h i w) -> p w h i", h=n, w=2)
-                .unsqueeze(4)
-                .to_broadcast([P, 2, n, HALF, 2]),
-                in1=factor[:, j]
-                .unsqueeze(2)
-                .to_broadcast([P, 2, n, DK])
-                .rearrange("p w h (i r) -> p w h i r", r=2),
+                out=products[:, 0],
+                in0=sums.rearrange("p (h d) -> p h d", h=n),
+                in1=cos[:, j].unsqueeze(1).to_broadcast([P, n, DK]),
+                op=MULT,
+            )
+            nc.vector.tensor_tensor(
+                out=products[:, 1].rearrange("p h (i r) -> p h i r", r=2),
+                in0=sums.rearrange("p (h i r) -> p h i r", h=n, r=2)[:, :, :, ::-1],
+                in1=sin[:, j].unsqueeze(1).to_broadcast([P, n, DK]).rearrange("p h (i r) -> p h i r", r=2),
                 op=MULT,
             )
             return products
@@ -160,7 +158,8 @@ def tile_multiheadselfattention_pa_k_kernel(tc, x, Wq, Wk, cos2, sin2, out_0, ou
 
         def store(out, heads, rotated):
             for b in range(B):
-                nc.sync.dma_start(
+                queue = nc.sync if b < B // 2 or out is out_0 else nc.scalar
+                queue.dma_start(
                     out=out[b, heads].rearrange("h (i j) d -> i h (j d)", j=J),
                     in_=rotated[b::B, heads].rearrange("p h j d -> p h (j d)"),
                 )
@@ -168,13 +167,6 @@ def tile_multiheadselfattention_pa_k_kernel(tc, x, Wq, Wk, cos2, sin2, out_0, ou
         all_heads = slice(0, H)
         q_rotated = out_pool.tile([P, H, J, DK], F32, name="q_rotated", tag="rotated")
         q_products = []
-
-        def rotate_q(step):
-            j = step // 2
-            if step % 2 == 0:
-                q_products.append(rotation_products(q_acc, j, all_heads))
-            else:
-                rotation_sum(nc.vector, q_rotated, j, all_heads, q_products[j])
 
         quantise_before = []
         ready = []
@@ -236,9 +228,15 @@ def tile_multiheadselfattention_pa_k_kernel(tc, x, Wq, Wk, cos2, sin2, out_0, ou
 
         def rotate_k_pass(g):
             if g == 0:
-                make_factor()
-            if g in ROTATE_PASSES:
-                rotate_q(ROTATE_PASSES.index(g))
+                make_tables()
+            if g == ROTATE_PASS:
+                for j in range(J):
+                    q_products.append(rotation_products(q_acc, j, all_heads))
+                    if j < J // 2:
+                        rotation_sum(nc.gpsimd, q_rotated, j, all_heads, q_products[j])
+            elif 0 < g - ROTATE_PASS <= J // 2:
+                j = g - ROTATE_PASS - 1 + J // 2
+                rotation_sum(nc.vector, q_rotated, j, all_heads, q_products[j])
 
         for first in range(0, PASSES, W_PASSES):
             w_unit(Wk, k_acc, first, VECTOR_COLS_K, rotate_k_pass)
@@ -247,18 +245,19 @@ def tile_multiheadselfattention_pa_k_kernel(tc, x, Wq, Wk, cos2, sin2, out_0, ou
 
         store(out_0, all_heads, q_rotated)
         k_rotated = out_pool.tile([P, H, J, DK], F32, name="k_rotated", tag="rotated")
-        halves = (slice(0, H // 2), slice(H // 2, H))
+        chunks = (slice(0, 6), slice(6, 12), slice(12, H))
         vector_sums = []
-        for half, heads in enumerate(halves):
+        for n, heads in enumerate(chunks):
             for j in range(J):
                 products = rotation_products(k_acc, j, heads)
                 if vector_sums:
                     rotation_sum(nc.vector, k_rotated, *vector_sums.pop(0))
-                if half == 1 and j == 0:
-                    store(out_1, halves[0], k_rotated)
-                if j < J - 2 * half:
+                if n > 0 and j == 0:
+                    store(out_1, chunks[n - 1], k_rotated)
+                if j < (3, 2, 1)[n]:
                     rotation_sum(nc.gpsimd, k_rotated, j, heads, products)
                 else:
                     vector_sums.append((j, heads, products))
-        rotation_sum(nc.vector, k_rotated, *vector_sums.pop(0))
-        store(out_1, halves[1], k_rotated)
+        while vector_sums:
+            rotation_sum(nc.vector, k_rotated, *vector_sums.pop(0))
+        store(out_1, chunks[-1], k_rotated)

from contextlib import ExitStack

import concourse.mybir as mybir
from concourse.masks import make_identity

F32 = mybir.dt.float32
BF16 = mybir.dt.bfloat16
U32 = mybir.dt.uint32
U8 = mybir.dt.uint8
FP8X4 = mybir.dt.float8_e4m3fn_x4
MULT = mybir.AluOpType.mult
ADD = mybir.AluOpType.add

B, S, D, H, DK = 4, 128, 8192, 16, 32
E = H * DK
HALF = DK // 2

P = 128
PACK = 4
K_PASS = P * PACK
PASSES = D // K_PASS
PSUM_BANKS = 8

J = B * S // P
X_PASSES = 8
X_LOADS = PASSES // X_PASSES
BANK_PASSES = 2
QUANT_PASSES = 4
W_PASSES = 2
EARLY_AFTER = (3, 6)

VECTOR_COLS_Q = 256
VECTOR_COLS_EARLY_Q = 320
VECTOR_COLS_K = 176
ROTATE_PASS = 3

FLOPS = 2 * B * S * D * 2 * E


def tile_multiheadselfattention_pa_k_kernel(tc, x, Wq, Wk, cos2, sin2, out_0, out_1):
    nc = tc.nc
    with ExitStack() as ctx:
        const = ctx.enter_context(tc.tile_pool(name="const", bufs=1))
        keep = ctx.enter_context(tc.tile_pool(name="keep", bufs=1))
        x_pool = ctx.enter_context(tc.tile_pool(name="x_raw", bufs=4))
        w_pool = ctx.enter_context(tc.tile_pool(name="w_raw", bufs=6))
        x_grouped_pool = ctx.enter_context(tc.tile_pool(name="x_grouped", bufs=4))
        w_grouped_pool = ctx.enter_context(tc.tile_pool(name="w_grouped", bufs=6))
        w_mx_pool = ctx.enter_context(tc.tile_pool(name="w_mx", bufs=8))
        rope_pool = ctx.enter_context(tc.tile_pool(name="rope", bufs=4))
        out_pool = ctx.enter_context(tc.tile_pool(name="rotated", bufs=2))
        banks = ctx.enter_context(tc.psum_pool(name="banks", bufs=PSUM_BANKS))
        ctx.enter_context(tc.manual_schedule())

        identity = const.tile([P, P], F32)
        make_identity(nc, identity[:])
        permutation = const.tile([P, P], F32)
        nc.gpsimd.tensor_copy(
            out=permutation[:].rearrange("p (i b) -> p b i", b=B),
            in_=identity[:].rearrange("p (b i) -> p b i", b=B),
        )
        cos_bf = const.tile([P, J, DK], BF16)
        sin_bf = const.tile([P, J, DK], BF16)
        for b in range(B):
            for table, source in ((cos_bf, cos2), (sin_bf, sin2)):
                nc.gpsimd.dma_start(
                    out=table[b::B].rearrange("p j d -> p (j d)"),
                    in_=source.rearrange("(i j) d -> i (j d)", j=J),
                )
        cos = const.tile([P, J, DK], F32)
        sin = const.tile([P, J, DK], F32)

        def make_tables():
            nc.vector.tensor_copy(out=cos[:], in_=cos_bf[:])
            pairs = sin[:].rearrange("p j (i r) -> p j r i", r=2)
            pairs_bf = sin_bf[:].rearrange("p j (i r) -> p j r i", r=2)
            nc.vector.tensor_scalar_mul(out=pairs[:, :, 0, :], in0=pairs_bf[:, :, 0, :], scalar1=-1.0)
            nc.vector.tensor_copy(out=pairs[:, :, 1, :], in_=pairs_bf[:, :, 1, :])

        x_codes = keep.tile([P, J, PASSES, P], U32, align_bytes=64)
        x_scales = keep.tile([P, J, PASSES, P], U8, align_bytes=64)

        x_rows = x.rearrange("b s k -> (b s) k").rearrange("(p j) k -> p j k", j=J)

        def transpose_bank(x_words, first_pass):
            xt = banks.tile([P, BANK_PASSES, 2, P], F32, name="xt", tag="bank")
            for i in range(BANK_PASSES):
                for u in range(2):
                    nc.tensor.transpose(
                        xt[:, i, u, :], x_words[:, first_pass + i, u, :], permutation[:]
                    )
            return xt

        def quantise_x(x_grouped, j, first_pass):
            passes = slice(first_pass, first_pass + QUANT_PASSES)
            nc.vector.quantize_mx(
                out=x_codes[:, j, passes].rearrange("p g s -> p (g s)").bitcast(FP8X4),
                scales=x_scales[:, j, passes].rearrange("p g s -> p (g s)"),
                in_=x_grouped[:].rearrange("p g s t -> p (g s t)"),
            )

        def group_w(w_raw, i, vector_cols):
            w_grouped = w_grouped_pool.tile([P, E, PACK], BF16, align_bytes=64)
            for copy, cols in (
                (nc.scalar.copy, slice(vector_cols, E)),
                (nc.vector.tensor_copy, slice(0, vector_cols)),
            ):
                copy(
                    out=w_grouped[:, cols, :].rearrange("p (c i) t -> p c t i", i=4),
                    in_=w_raw[:, i, :, cols].rearrange("p t (c i) -> p c t i", i=4),
                )
            return w_grouped

        def quantise_w(w_grouped):
            w_codes = w_mx_pool.tile([P, E], U32, align_bytes=64)
            w_scales = w_mx_pool.tile([P, E], U8, align_bytes=64)
            nc.vector.quantize_mx(
                out=w_codes[:].bitcast(FP8X4),
                scales=w_scales[:],
                in_=w_grouped[:].rearrange("p n t -> p (n t)"),
            )
            return w_codes, w_scales

        def multiply(acc, g, w_codes, w_scales):
            for j in range(J):
                nc.tensor.matmul_mx(
                    out=acc[j][:],
                    lhsT=x_codes[:, j, g, :].bitcast(FP8X4),
                    lhsT_scale=x_scales[:, j, g, :],
                    rhs=w_codes[:].bitcast(FP8X4),
                    rhs_scale=w_scales[:],
                    start=(g == 0),
                    stop=(g == PASSES - 1),
                )

        def rotation_products(acc, j, heads):
            n = heads.stop - heads.start
            products = rope_pool.tile([P, 2, n, DK], F32, name="products")
            sums = acc[j][:, heads.start * DK : heads.stop * DK]
            nc.vector.tensor_tensor(
                out=products[:, 0],
                in0=sums.rearrange("p (h d) -> p h d", h=n),
                in1=cos[:, j].unsqueeze(1).to_broadcast([P, n, DK]),
                op=MULT,
            )
            nc.vector.tensor_tensor(
                out=products[:, 1].rearrange("p h (i r) -> p h i r", r=2),
                in0=sums.rearrange("p (h i r) -> p h i r", h=n, r=2)[:, :, :, ::-1],
                in1=sin[:, j].unsqueeze(1).to_broadcast([P, n, DK]).rearrange("p h (i r) -> p h i r", r=2),
                op=MULT,
            )
            return products

        def rotation_sum(engine, rotated, j, heads, products):
            engine.tensor_tensor(
                out=rotated[:, heads, j, :], in0=products[:, 0], in1=products[:, 1], op=ADD
            )

        def store(out, heads, rotated):
            for b in range(B):
                queue = nc.sync if b < B // 2 or out is out_0 else nc.scalar
                queue.dma_start(
                    out=out[b, heads].rearrange("h (i j) d -> i h (j d)", j=J),
                    in_=rotated[b::B, heads].rearrange("p h j d -> p h (j d)"),
                )

        all_heads = slice(0, H)
        q_rotated = out_pool.tile([P, H, J, DK], F32, name="q_rotated", tag="rotated")
        q_products = []

        quantise_before = []
        ready = []

        def quantise_next():
            while quantise_before:
                quantise_before.pop(0)()

        def x_unit(j, load):
            x_raw = x_pool.tile([P, X_PASSES * K_PASS], BF16)
            pieces = X_PASSES // BANK_PASSES if j == 0 and load == 0 else 1
            width = X_PASSES * K_PASS // pieces
            for piece in range(pieces):
                first_k = load * X_PASSES * K_PASS + piece * width
                nc.sync.dma_start(
                    out=x_raw[:, piece * width : (piece + 1) * width],
                    in_=x_rows[:, j, first_k : first_k + width],
                )
            x_words = x_raw[:].bitcast(F32).rearrange("s (g p u) -> s g u p", p=P, u=2)
            for first in range(0, X_PASSES, QUANT_PASSES):
                x_grouped = x_grouped_pool.tile([P, QUANT_PASSES, P, PACK], BF16, align_bytes=64)
                for i in range(0, QUANT_PASSES, BANK_PASSES):
                    xt = transpose_bank(x_words, first + i)
                    nc.scalar.copy(
                        out=x_grouped[:].bitcast(F32)[:, i : i + BANK_PASSES],
                        in_=xt[:].rearrange("p g u s -> p g s u"),
                    )
                quantise_next()
                quantise_before.append(lambda a=x_grouped, b=load * X_PASSES + first: quantise_x(a, j, b))

        def w_unit(w, acc, first, vector_cols, rotate):
            w_raw = w_pool.tile([P, W_PASSES, PACK, E], BF16)
            nc.sync.dma_start(
                out=w_raw[:].rearrange("p g t n -> p g (t n)"),
                in_=w.rearrange("(g p t) n -> p g (t n)", p=P, t=PACK)[:, first : first + W_PASSES, :],
            )
            for i in range(W_PASSES):
                g = first + i
                w_grouped = group_w(w_raw, i, vector_cols)
                quantise_next()
                quantise_before.append(lambda a=w_grouped, b=g: ready.append((b, *quantise_w(a))))
                if acc is not None:
                    while ready:
                        multiply(acc, *ready.pop(0))
                rotate(g)

        early = 0
        for n in range(J * X_LOADS):
            x_unit(n // X_LOADS, n % X_LOADS)
            if n in EARLY_AFTER:
                w_unit(Wq, None, early, VECTOR_COLS_EARLY_Q, lambda g: None)
                early += W_PASSES
        q_acc = [banks.tile([P, E], F32, name="q_acc%d" % j, tag="bank") for j in range(J)]
        k_acc = [banks.tile([P, E], F32, name="k_acc%d" % j, tag="bank") for j in range(J)]
        for first in range(early, PASSES, W_PASSES):
            w_unit(Wq, q_acc, first, VECTOR_COLS_Q, lambda g: None)
        quantise_next()
        multiply(q_acc, *ready.pop(0))

        def rotate_k_pass(g):
            if g == 0:
                make_tables()
            if g == ROTATE_PASS:
                for j in range(J):
                    q_products.append(rotation_products(q_acc, j, all_heads))
                    if j < J // 2:
                        rotation_sum(nc.gpsimd, q_rotated, j, all_heads, q_products[j])
            elif 0 < g - ROTATE_PASS <= J // 2:
                j = g - ROTATE_PASS - 1 + J // 2
                rotation_sum(nc.vector, q_rotated, j, all_heads, q_products[j])

        for first in range(0, PASSES, W_PASSES):
            w_unit(Wk, k_acc, first, VECTOR_COLS_K, rotate_k_pass)
        quantise_next()
        multiply(k_acc, *ready.pop(0))

        store(out_0, all_heads, q_rotated)
        k_rotated = out_pool.tile([P, H, J, DK], F32, name="k_rotated", tag="rotated")
        chunks = (slice(0, 6), slice(6, 12), slice(12, H))
        vector_sums = []
        for n, heads in enumerate(chunks):
            for j in range(J):
                products = rotation_products(k_acc, j, heads)
                if vector_sums:
                    rotation_sum(nc.vector, k_rotated, *vector_sums.pop(0))
                if n > 0 and j == 0:
                    store(out_1, chunks[n - 1], k_rotated)
                if j < (3, 2, 1)[n]:
                    rotation_sum(nc.gpsimd, k_rotated, j, heads, products)
                else:
                    vector_sums.append((j, heads, products))
        while vector_sums:
            rotation_sum(nc.vector, k_rotated, *vector_sums.pop(0))
        store(out_1, chunks[-1], k_rotated)
